import numpy as np
import ml_dtypes


def mxq(x, axis, fmt="e4m3"):
    dtype, down = {"e4m3": (ml_dtypes.float8_e4m3fn, 7), "e5m2": (ml_dtypes.float8_e5m2, 14)}[fmt]
    v = np.moveaxis(np.asarray(x, np.float32).astype(ml_dtypes.bfloat16).astype(np.float64), axis, -1)
    blocks = v.reshape(v.shape[:-1] + (-1, 32))
    amax = np.abs(blocks).max(-1, keepdims=True)
    byte = np.maximum(np.where(amax > 0, np.frexp(amax)[1] - 1 + 127, 0) - down, 1)
    scale = np.exp2(byte - 127.0)
    codes = (blocks / scale).astype(np.float32).astype(dtype).astype(np.float64)
    return np.moveaxis((codes * scale).reshape(v.shape), -1, axis)


WIDE = False


def mx_kscale(k):
    if not WIDE:
        return np.ones(k)
    levels = np.array([20, -20, 10, -10, 0])
    a = np.random.permutation(np.resize(levels, k // 512 * 4)).reshape(k // 512, 4)
    idx = np.arange(k)
    return np.exp2(a[idx // 512, idx % 128 // 32])


BF16 = ml_dtypes.bfloat16


def bf(x):
    return np.asarray(x, np.float32).astype(BF16)


def f64(x):
    return np.asarray(x).astype(np.float64)


B, D = 2048, 1024


def setup_inputs():
    s = mx_kscale(B)[:, None]
    x = np.random.standard_normal((B, D)) * s
    W = np.random.standard_normal((D, D)) * 0.04
    b = np.random.standard_normal(D) * 0.5
    g = np.random.standard_normal((B, D)) * np.exp2(np.random.randint(-12, 1, (B, 1))) / s
    return {"x": bf(x), "W": bf(W), "b": bf(b), "grad_out": bf(g)}


def reference(x, W, b, grad_out):
    d = W.shape[0]
    mask = np.tril(np.ones((d, d), dtype=np.float64), k=-1)
    full = mxq(f64(grad_out), 0, "e5m2").T @ mxq(f64(x), 0, "e4m3")
    return full * mask

@@ -1,0 +1,157 @@
+from contextlib import ExitStack
+
+import concourse.mybir as mybir
+
+BF16 = mybir.dt.bfloat16
+F32 = mybir.dt.float32
+U32 = mybir.dt.uint32
+U8 = mybir.dt.uint8
+E4M3X4 = mybir.dt.float8_e4m3fn_x4
+E5M2X4 = mybir.dt.float8_e5m2_x4
+ALU = mybir.AluOpType
+
+P = 128
+PACK = 4
+K_PASS = P * PACK
+TOKENS = 2048
+D = 1024
+PASSES = TOKENS // K_PASS
+UNIT = 512
+V_COLS = 248
+
+FLOPS = 2 * TOKENS * D * D
+BYTES = 2 * TOKENS * D * 2 + D * D * 4
+
+
+def tile_fvsbn_kernel(tc, x, W, b, grad_out, out):
+    nc = tc.nc
+    with ExitStack() as ctx:
+        raw_pool = ctx.enter_context(tc.tile_pool(name="raw", bufs=1))
+        grp_pool = ctx.enter_context(tc.tile_pool(name="grp", bufs=4))
+        keep = ctx.enter_context(tc.tile_pool(name="keep", bufs=1))
+        psum = ctx.enter_context(tc.psum_pool(name="psum", bufs=1))
+        ctx.enter_context(tc.manual_schedule())
+
+        mask = keep.tile([P, UNIT], F32, name="mask")
+        nc.gpsimd.memset(mask[:], 1.0)
+        nc.gpsimd.affine_select(
+            out=mask[:],
+            in_=mask[:],
+            pattern=[[-1, UNIT]],
+            compare_op=ALU.is_gt,
+            fill=0.0,
+            base=UNIT - P,
+            channel_multiplier=1,
+        )
+        zero = keep.tile([P, D - P], F32, name="zero")
+        nc.gpsimd.memset(zero[:], 0.0)
+
+        dram = {"x": x, "g": grad_out}
+        fmt = {"x": E4M3X4, "g": E5M2X4}
+        raw = {}
+        units = []
+        for c in range(PASSES):
+            for o in ("x", "g"):
+                rows = dram[o][c * K_PASS : (c + 1) * K_PASS, :]
+                split = (c == 0 and o == "x") or (c == PASSES - 1 and o == "g")
+                if split:
+                    for h in range(2):
+                        half = raw_pool.tile([P, PACK, UNIT], BF16, name="raw_%s%d%d" % (o, c, h))
+                        nc.sync.dma_start(
+                            out=half[:],
+                            in_=rows[:, h * UNIT : (h + 1) * UNIT].rearrange("(p j) w -> p j w", j=PACK),
+                        )
+                        raw[(o, c, h)] = half[:]
+                else:
+                    whole = raw_pool.tile([P, PACK, D], BF16, name="raw_%s%d" % (o, c))
+                    nc.sync.dma_start(out=whole[:], in_=rows.rearrange("(p j) w -> p j w", j=PACK))
+                    for h in range(2):
+                        raw[(o, c, h)] = whole[:, :, h * UNIT : (h + 1) * UNIT]
+                units.append((o, c, 0))
+                units.append((o, c, 1))
+
+        for m in range(D // P - 1):
+            first = (m + 1) * P
+            nc.sync.dma_start(out=out[m * P : (m + 1) * P, first:D], in_=zero[:, 0 : D - first])
+
+        grouped = {}
+        codes = {}
+        scales = {}
+        acc = {}
+
+        def regroup(u):
+            src = raw[u]
+            dst = grp_pool.tile([P, UNIT, PACK], BF16, name="grouped", tag="grouped", align_bytes=64)
+            grouped[u] = dst
+            nc.vector.tensor_copy(
+                out=dst[:, 0:V_COLS, :].rearrange("p (c i) t -> p c t i", i=4),
+                in_=src[:, :, 0:V_COLS].rearrange("p t (c i) -> p c t i", i=4),
+            )
+            nc.scalar.copy(
+                out=dst[:, V_COLS:UNIT, :].rearrange("p (c i) t -> p c t i", i=4),
+                in_=src[:, :, V_COLS:UNIT].rearrange("p t (c i) -> p c t i", i=4),
+            )
+
+        def quantise(u):
+            o, c, h = u
+            codes[u] = keep.tile([P, UNIT], U32, name="codes_%s%d%d" % u, align_bytes=64)
+            scales[u] = keep.tile([P, UNIT], U8, name="scales_%s%d%d" % u, align_bytes=64)
+            nc.vector.quantize_mx(
+                out=codes[u][:].bitcast(fmt[o]),
+                scales=scales[u][:],
+                in_=grouped[u][:].rearrange("p w t -> p (w t)"),
+            )
+
+        def mx_pass(bank, c, m, h):
+            gu = ("g", c, m // 4)
+            xu = ("x", c, h)
+            cols = slice((m % 4) * P, (m % 4 + 1) * P)
+            nc.tensor.matmul_mx(
+                out=bank[:],
+                lhsT=codes[gu][:, cols].bitcast(E5M2X4),
+                lhsT_scale=scales[gu][:, cols],
+                rhs=codes[xu][:].bitcast(E4M3X4),
+                rhs_scale=scales[xu][:],
+                start=(c == 0),
+                stop=(c == PASSES - 1),
+            )
+
+        for m in range(8):
+            acc[m] = psum.tile([P, UNIT], F32, name="acc_lo%d" % m, tag="bank%d" % m)
+
+        for i in range(len(units) + 1):
+            if i < len(units):
+                regroup(units[i])
+            if i >= 1:
+                u = units[i - 1]
+                quantise(u)
+                if u[0] == "g":
+                    for m in range(4 * u[2], 4 * u[2] + 4):
+                        mx_pass(acc[m], u[1], m, 0)
+
+        def leave_masked(bank, m, first_col, width, label):
+            res = keep.tile([P, width], F32, name="res_%s%d" % (label, m))
+            nc.vector.tensor_tensor(
+                out=res[:], in0=bank[:, 0:width], in1=mask[:, UNIT - width : UNIT], op=ALU.mult
+            )
+            return res, out[m * P : (m + 1) * P, first_col : first_col + width]
+
+        def leave_plain(bank, m):
+            res = keep.tile([P, UNIT], F32, name="res_b%d" % m)
+            nc.scalar.copy(out=res[:], in_=bank[:])
+            return res, out[m * P : (m + 1) * P, 0:UNIT]
+
+        ready = {}
+        for m in range(4):
+            ready[m] = leave_masked(acc[m], m, 0, (m + 1) * P, "a")
+        for m in range(4, 8):
+            ready[m] = leave_plain(acc[m], m)
+        for m in (0, 1, 4, 2, 5, 3, 6, 7):
+            nc.sync.dma_start(out=ready[m][1], in_=ready[m][0][:])
+
+        for k, m in enumerate((7, 6, 5, 4)):
+            bank = psum.tile([P, UNIT], F32, name="acc_hi%d" % m, tag="bank%d" % k)
+            for c in range(PASSES):
+                mx_pass(bank, c, m, 1)
+            res, where = leave_masked(bank, m, UNIT, (m - 3) * P, "c")
+            nc.sync.dma_start(out=where, in_=res[:])

@@ -53,7 +53,7 @@ def tile_fvsbn_kernel(tc, x, W, b, grad_out, out):
         for c in range(PASSES):
             for o in ("x", "g"):
                 rows = dram[o][c * K_PASS : (c + 1) * K_PASS, :]
-                split = (c == 0 and o == "x") or (c == PASSES - 1 and o == "g")
+                split = False
                 if split:
                     for h in range(2):
                         half = raw_pool.tile([P, PACK, UNIT], BF16, name="raw_%s%d%d" % (o, c, h))

@@ -17,7 +17,7 @@ TOKENS = 2048
 D = 1024
 PASSES = TOKENS // K_PASS
 UNIT = 512
-V_COLS = 248
+V_COLS = 264
 
 FLOPS = 2 * TOKENS * D * D
 BYTES = 2 * TOKENS * D * 2 + D * D * 4

@@ -17,7 +17,7 @@ TOKENS = 2048
 D = 1024
 PASSES = TOKENS // K_PASS
 UNIT = 512
-V_COLS = 264
+V_COLS = 248
 
 FLOPS = 2 * TOKENS * D * D
 BYTES = 2 * TOKENS * D * 2 + D * D * 4
@@ -27,7 +27,7 @@ def tile_fvsbn_kernel(tc, x, W, b, grad_out, out):
     nc = tc.nc
     with ExitStack() as ctx:
         raw_pool = ctx.enter_context(tc.tile_pool(name="raw", bufs=1))
-        grp_pool = ctx.enter_context(tc.tile_pool(name="grp", bufs=4))
+        grp_pool = ctx.enter_context(tc.tile_pool(name="grp", bufs=6))
         keep = ctx.enter_context(tc.tile_pool(name="keep", bufs=1))
         psum = ctx.enter_context(tc.psum_pool(name="psum", bufs=1))
         ctx.enter_context(tc.manual_schedule())
@@ -50,25 +50,32 @@ def tile_fvsbn_kernel(tc, x, W, b, grad_out, out):
         fmt = {"x": E4M3X4, "g": E5M2X4}
         raw = {}
         units = []
-        for c in range(PASSES):
+        def load(o, c, halves):
+            rows = dram[o][c * K_PASS : (c + 1) * K_PASS, :]
+            if len(halves) == 2:
+                whole = raw_pool.tile([P, PACK, D], BF16, name="raw_%s%d" % (o, c))
+                nc.sync.dma_start(out=whole[:], in_=rows.rearrange("(p j) w -> p j w", j=PACK))
+                for h in halves:
+                    raw[(o, c, h)] = whole[:, :, h * UNIT : (h + 1) * UNIT]
+            else:
+                h = halves[0]
+                half = raw_pool.tile([P, PACK, UNIT], BF16, name="raw_%s%d%d" % (o, c, h))
+                nc.sync.dma_start(
+                    out=half[:],
+                    in_=rows[:, h * UNIT : (h + 1) * UNIT].rearrange("(p j) w -> p j w", j=PACK),
+                )
+                raw[(o, c, h)] = half[:]
+
+        for c in range(PASSES - 1):
             for o in ("x", "g"):
-                rows = dram[o][c * K_PASS : (c + 1) * K_PASS, :]
-                split = False
-                if split:
-                    for h in range(2):
-                        half = raw_pool.tile([P, PACK, UNIT], BF16, name="raw_%s%d%d" % (o, c, h))
-                        nc.sync.dma_start(
-                            out=half[:],
-                            in_=rows[:, h * UNIT : (h + 1) * UNIT].rearrange("(p j) w -> p j w", j=PACK),
-                        )
-                        raw[(o, c, h)] = half[:]
-                else:
-                    whole = raw_pool.tile([P, PACK, D], BF16, name="raw_%s%d" % (o, c))
-                    nc.sync.dma_start(out=whole[:], in_=rows.rearrange("(p j) w -> p j w", j=PACK))
-                    for h in range(2):
-                        raw[(o, c, h)] = whole[:, :, h * UNIT : (h + 1) * UNIT]
+                load(o, c, (0, 1))
                 units.append((o, c, 0))
                 units.append((o, c, 1))
+        last = PASSES - 1
+        load("x", last, (0,))
+        load("g", last, (0, 1))
+        load("x", last, (1,))
+        units.extend([("x", last, 0), ("g", last, 0), ("g", last, 1), ("x", last, 1)])
 
         for m in range(D // P - 1):
             first = (m + 1) * P
@@ -119,9 +126,20 @@ def tile_fvsbn_kernel(tc, x, W, b, grad_out, out):
         for m in range(8):
             acc[m] = psum.tile([P, UNIT], F32, name="acc_lo%d" % m, tag="bank%d" % m)
 
-        for i in range(len(units) + 1):
-            if i < len(units):
-                regroup(units[i])
+        def leave_masked(bank, m, first_col, width, label):
+            res = keep.tile([P, width], F32, name="res_%s%d" % (label, m))
+            nc.vector.tensor_tensor(
+                out=res[:], in0=bank[:, 0:width], in1=mask[:, UNIT - width : UNIT], op=ALU.mult
+            )
+            nc.sync.dma_start(out=out[m * P : (m + 1) * P, first_col : first_col + width], in_=res[:])
+
+        def leave_plain(bank, m):
+            res = keep.tile([P, UNIT], F32, name="res_b%d" % m)
+            nc.scalar.copy(out=res[:], in_=bank[:])
+            nc.sync.dma_start(out=out[m * P : (m + 1) * P, 0:UNIT], in_=res[:])
+
+        for i in range(len(units)):
+            regroup(units[i])
             if i >= 1:
                 u = units[i - 1]
                 quantise(u)
@@ -129,29 +147,21 @@ def tile_fvsbn_kernel(tc, x, W, b, grad_out, out):
                     for m in range(4 * u[2], 4 * u[2] + 4):
                         mx_pass(acc[m], u[1], m, 0)
 
-        def leave_masked(bank, m, first_col, width, label):
-            res = keep.tile([P, width], F32, name="res_%s%d" % (label, m))
-            nc.vector.tensor_tensor(
-                out=res[:], in0=bank[:, 0:width], in1=mask[:, UNIT - width : UNIT], op=ALU.mult
-            )
-            return res, out[m * P : (m + 1) * P, first_col : first_col + width]
-
-        def leave_plain(bank, m):
-            res = keep.tile([P, UNIT], F32, name="res_b%d" % m)
-            nc.scalar.copy(out=res[:], in_=bank[:])
-            return res, out[m * P : (m + 1) * P, 0:UNIT]
-
-        ready = {}
         for m in range(4):
-            ready[m] = leave_masked(acc[m], m, 0, (m + 1) * P, "a")
+            leave_masked(acc[m], m, 0, (m + 1) * P, "a")
+        quantise(units[-1])
         for m in range(4, 8):
-            ready[m] = leave_plain(acc[m], m)
-        for m in (0, 1, 4, 2, 5, 3, 6, 7):
-            nc.sync.dma_start(out=ready[m][1], in_=ready[m][0][:])
+            leave_plain(acc[m], m)
 
+        hi_bank = {}
         for k, m in enumerate((7, 6, 5, 4)):
-            bank = psum.tile([P, UNIT], F32, name="acc_hi%d" % m, tag="bank%d" % k)
-            for c in range(PASSES):
-                mx_pass(bank, c, m, 1)
-            res, where = leave_masked(bank, m, UNIT, (m - 3) * P, "c")
-            nc.sync.dma_start(out=where, in_=res[:])
+            hi_bank[m] = psum.tile([P, UNIT], F32, name="acc_hi%d" % m, tag="bank%d" % k)
+        for m in (7, 6, 5):
+            for c in range(PASSES - 1):
+                mx_pass(hi_bank[m], c, m, 1)
+        for m in (7, 6, 5):
+            mx_pass(hi_bank[m], last, m, 1)
+            leave_masked(hi_bank[m], m, UNIT, (m - 3) * P, "c")
+        for c in range(PASSES):
+            mx_pass(hi_bank[4], c, 4, 1)
+        leave_masked(hi_bank[4], 4, UNIT, P, "c")

@@ -86,17 +86,21 @@ def tile_fvsbn_kernel(tc, x, W, b, grad_out, out):
         scales = {}
         acc = {}
 
-        def regroup(u):
-            src = raw[u]
-            dst = grp_pool.tile([P, UNIT, PACK], BF16, name="grouped", tag="grouped", align_bytes=64)
-            grouped[u] = dst
+        def grouped_tile(u):
+            if u not in grouped:
+                grouped[u] = grp_pool.tile([P, UNIT, PACK], BF16, name="grouped", tag="grouped", align_bytes=64)
+            return grouped[u]
+
+        def regroup_v(u):
             nc.vector.tensor_copy(
-                out=dst[:, 0:V_COLS, :].rearrange("p (c i) t -> p c t i", i=4),
-                in_=src[:, :, 0:V_COLS].rearrange("p t (c i) -> p c t i", i=4),
+                out=grouped_tile(u)[:, 0:V_COLS, :].rearrange("p (c i) t -> p c t i", i=4),
+                in_=raw[u][:, :, 0:V_COLS].rearrange("p t (c i) -> p c t i", i=4),
             )
+
+        def regroup_s(u):
             nc.scalar.copy(
-                out=dst[:, V_COLS:UNIT, :].rearrange("p (c i) t -> p c t i", i=4),
-                in_=src[:, :, V_COLS:UNIT].rearrange("p t (c i) -> p c t i", i=4),
+                out=grouped_tile(u)[:, V_COLS:UNIT, :].rearrange("p (c i) t -> p c t i", i=4),
+                in_=raw[u][:, :, V_COLS:UNIT].rearrange("p t (c i) -> p c t i", i=4),
             )
 
         def quantise(u):
@@ -138,30 +142,41 @@ def tile_fvsbn_kernel(tc, x, W, b, grad_out, out):
             nc.scalar.copy(out=res[:], in_=bank[:])
             nc.sync.dma_start(out=out[m * P : (m + 1) * P, 0:UNIT], in_=res[:])
 
-        for i in range(len(units)):
-            regroup(units[i])
-            if i >= 1:
-                u = units[i - 1]
-                quantise(u)
-                if u[0] == "g":
-                    for m in range(4 * u[2], 4 * u[2] + 4):
-                        mx_pass(acc[m], u[1], m, 0)
+        def quantise_and_multiply(u):
+            quantise(u)
+            if u[0] == "g":
+                for m in range(4 * u[2], 4 * u[2] + 4):
+                    mx_pass(acc[m], u[1], m, 0)
 
+        steady = len(units) - 2
+        for i in range(steady):
+            regroup_v(units[i])
+            regroup_s(units[i])
+            if i >= 1:
+                quantise_and_multiply(units[i - 1])
+        g_lo, g_hi, x_hi = units[steady - 1], units[steady], units[steady + 1]
+        regroup_s(g_hi)
+        quantise_and_multiply(g_lo)
+        regroup_v(g_hi)
+        regroup_s(x_hi)
+        quantise_and_multiply(g_hi)
         for m in range(4):
             leave_masked(acc[m], m, 0, (m + 1) * P, "a")
-        quantise(units[-1])
+        regroup_v(x_hi)
+        quantise(x_hi)
         for m in range(4, 8):
             leave_plain(acc[m], m)
 
         hi_bank = {}
         for k, m in enumerate((7, 6, 5, 4)):
             hi_bank[m] = psum.tile([P, UNIT], F32, name="acc_hi%d" % m, tag="bank%d" % k)
-        for m in (7, 6, 5):
+        for m in (7, 6):
             for c in range(PASSES - 1):
                 mx_pass(hi_bank[m], c, m, 1)
-        for m in (7, 6, 5):
+        for m in (7, 6):
             mx_pass(hi_bank[m], last, m, 1)
             leave_masked(hi_bank[m], m, UNIT, (m - 3) * P, "c")
-        for c in range(PASSES):
-            mx_pass(hi_bank[4], c, 4, 1)
-        leave_masked(hi_bank[4], 4, UNIT, P, "c")
+        for m in (5, 4):
+            for c in range(PASSES):
+                mx_pass(hi_bank[m], c, m, 1)
+            leave_masked(hi_bank[m], m, UNIT, (m - 3) * P, "c")

from contextlib import ExitStack

import concourse.mybir as mybir

BF16 = mybir.dt.bfloat16
F32 = mybir.dt.float32
U32 = mybir.dt.uint32
U8 = mybir.dt.uint8
E4M3X4 = mybir.dt.float8_e4m3fn_x4
E5M2X4 = mybir.dt.float8_e5m2_x4
ALU = mybir.AluOpType

P = 128
PACK = 4
K_PASS = P * PACK
TOKENS = 2048
D = 1024
PASSES = TOKENS // K_PASS
UNIT = 512
V_COLS = 248

FLOPS = 2 * TOKENS * D * D
BYTES = 2 * TOKENS * D * 2 + D * D * 4


def tile_fvsbn_kernel(tc, x, W, b, grad_out, out):
    nc = tc.nc
    with ExitStack() as ctx:
        raw_pool = ctx.enter_context(tc.tile_pool(name="raw", bufs=1))
        grp_pool = ctx.enter_context(tc.tile_pool(name="grp", bufs=6))
        keep = ctx.enter_context(tc.tile_pool(name="keep", bufs=1))
        psum = ctx.enter_context(tc.psum_pool(name="psum", bufs=1))
        ctx.enter_context(tc.manual_schedule())

        mask = keep.tile([P, UNIT], F32, name="mask")
        nc.gpsimd.memset(mask[:], 1.0)
        nc.gpsimd.affine_select(
            out=mask[:],
            in_=mask[:],
            pattern=[[-1, UNIT]],
            compare_op=ALU.is_gt,
            fill=0.0,
            base=UNIT - P,
            channel_multiplier=1,
        )
        zero = keep.tile([P, D - P], F32, name="zero")
        nc.gpsimd.memset(zero[:], 0.0)

        dram = {"x": x, "g": grad_out}
        fmt = {"x": E4M3X4, "g": E5M2X4}
        raw = {}
        units = []
        def load(o, c, halves):
            rows = dram[o][c * K_PASS : (c + 1) * K_PASS, :]
            if len(halves) == 2:
                whole = raw_pool.tile([P, PACK, D], BF16, name="raw_%s%d" % (o, c))
                nc.sync.dma_start(out=whole[:], in_=rows.rearrange("(p j) w -> p j w", j=PACK))
                for h in halves:
                    raw[(o, c, h)] = whole[:, :, h * UNIT : (h + 1) * UNIT]
            else:
                h = halves[0]
                half = raw_pool.tile([P, PACK, UNIT], BF16, name="raw_%s%d%d" % (o, c, h))
                nc.sync.dma_start(
                    out=half[:],
                    in_=rows[:, h * UNIT : (h + 1) * UNIT].rearrange("(p j) w -> p j w", j=PACK),
                )
                raw[(o, c, h)] = half[:]

        for c in range(PASSES - 1):
            for o in ("x", "g"):
                load(o, c, (0, 1))
                units.append((o, c, 0))
                units.append((o, c, 1))
        last = PASSES - 1
        load("x", last, (0,))
        load("g", last, (0, 1))
        load("x", last, (1,))
        units.extend([("x", last, 0), ("g", last, 0), ("g", last, 1), ("x", last, 1)])

        for m in range(D // P - 1):
            first = (m + 1) * P
            nc.sync.dma_start(out=out[m * P : (m + 1) * P, first:D], in_=zero[:, 0 : D - first])

        grouped = {}
        codes = {}
        scales = {}
        acc = {}

        def grouped_tile(u):
            if u not in grouped:
                grouped[u] = grp_pool.tile([P, UNIT, PACK], BF16, name="grouped", tag="grouped", align_bytes=64)
            return grouped[u]

        def regroup_v(u):
            nc.vector.tensor_copy(
                out=grouped_tile(u)[:, 0:V_COLS, :].rearrange("p (c i) t -> p c t i", i=4),
                in_=raw[u][:, :, 0:V_COLS].rearrange("p t (c i) -> p c t i", i=4),
            )

        def regroup_s(u):
            nc.scalar.copy(
                out=grouped_tile(u)[:, V_COLS:UNIT, :].rearrange("p (c i) t -> p c t i", i=4),
                in_=raw[u][:, :, V_COLS:UNIT].rearrange("p t (c i) -> p c t i", i=4),
            )

        def quantise(u):
            o, c, h = u
            codes[u] = keep.tile([P, UNIT], U32, name="codes_%s%d%d" % u, align_bytes=64)
            scales[u] = keep.tile([P, UNIT], U8, name="scales_%s%d%d" % u, align_bytes=64)
            nc.vector.quantize_mx(
                out=codes[u][:].bitcast(fmt[o]),
                scales=scales[u][:],
                in_=grouped[u][:].rearrange("p w t -> p (w t)"),
            )

        def mx_pass(bank, c, m, h):
            gu = ("g", c, m // 4)
            xu = ("x", c, h)
            cols = slice((m % 4) * P, (m % 4 + 1) * P)
            nc.tensor.matmul_mx(
                out=bank[:],
                lhsT=codes[gu][:, cols].bitcast(E5M2X4),
                lhsT_scale=scales[gu][:, cols],
                rhs=codes[xu][:].bitcast(E4M3X4),
                rhs_scale=scales[xu][:],
                start=(c == 0),
                stop=(c == PASSES - 1),
            )

        for m in range(8):
            acc[m] = psum.tile([P, UNIT], F32, name="acc_lo%d" % m, tag="bank%d" % m)

        def leave_masked(bank, m, first_col, width, label):
            res = keep.tile([P, width], F32, name="res_%s%d" % (label, m))
            nc.vector.tensor_tensor(
                out=res[:], in0=bank[:, 0:width], in1=mask[:, UNIT - width : UNIT], op=ALU.mult
            )
            nc.sync.dma_start(out=out[m * P : (m + 1) * P, first_col : first_col + width], in_=res[:])

        def leave_plain(bank, m):
            res = keep.tile([P, UNIT], F32, name="res_b%d" % m)
            nc.scalar.copy(out=res[:], in_=bank[:])
            nc.sync.dma_start(out=out[m * P : (m + 1) * P, 0:UNIT], in_=res[:])

        def quantise_and_multiply(u):
            quantise(u)
            if u[0] == "g":
                for m in range(4 * u[2], 4 * u[2] + 4):
                    mx_pass(acc[m], u[1], m, 0)

        steady = len(units) - 2
        for i in range(steady):
            regroup_v(units[i])
            regroup_s(units[i])
            if i >= 1:
                quantise_and_multiply(units[i - 1])
        g_lo, g_hi, x_hi = units[steady - 1], units[steady], units[steady + 1]
        regroup_s(g_hi)
        quantise_and_multiply(g_lo)
        regroup_v(g_hi)
        regroup_s(x_hi)
        quantise_and_multiply(g_hi)
        for m in range(4):
            leave_masked(acc[m], m, 0, (m + 1) * P, "a")
        regroup_v(x_hi)
        quantise(x_hi)
        for m in range(4, 8):
            leave_plain(acc[m], m)

        hi_bank = {}
        for k, m in enumerate((7, 6, 5, 4)):
            hi_bank[m] = psum.tile([P, UNIT], F32, name="acc_hi%d" % m, tag="bank%d" % k)
        for m in (7, 6):
            for c in range(PASSES - 1):
                mx_pass(hi_bank[m], c, m, 1)
        for m in (7, 6):
            mx_pass(hi_bank[m], last, m, 1)
            leave_masked(hi_bank[m], m, UNIT, (m - 3) * P, "c")
        for m in (5, 4):
            for c in range(PASSES):
                mx_pass(hi_bank[m], c, m, 1)
            leave_masked(hi_bank[m], m, UNIT, (m - 3) * P, "c")
